import numpy as np
import ml_dtypes

BF16 = ml_dtypes.bfloat16


def bf(x):
    return np.asarray(x, np.float32).astype(BF16)


def f32(x):
    return np.asarray(x, np.float32)


def f64(x):
    return np.asarray(x).astype(np.float64)


def striped(idx):
    return np.tile(idx.reshape(-1, 16).T, (8, 1))


C, F, S, N = 256, 1024, 4096, 512
ERF_TERMS, ERF_LIM, W2_SCALE, BIAS_SCALE = 150, 6.0, 1.5, 0.1


def erf(a):
    a = np.asarray(a, np.float64)
    c = np.clip(a, -ERF_LIM, ERF_LIM)
    term = c.copy()
    tot = c.copy()
    for n in range(1, ERF_TERMS):
        term = term * 2.0 * c * c / (2 * n + 1)
        tot = tot + term
    r = 2.0 / np.sqrt(np.pi) * np.exp(-c * c) * tot
    return np.where(np.abs(a) > ERF_LIM, np.sign(a), r)


def gelu_erf(v):
    return 0.5 * v * (1.0 + erf(v / np.sqrt(2.0)))


def setup_inputs():
    x = np.random.standard_normal((C, N))
    x = (x - x.mean(0, keepdims=True)) / np.sqrt(x.var(0, keepdims=True))
    return {"base": f32(np.random.standard_normal((C, S))), "x": f32(x), "w1": bf(np.random.standard_normal((C, F)) / np.sqrt(C)), "b1": f32(BIAS_SCALE * np.random.standard_normal((F, 1))), "w2": bf(W2_SCALE * np.random.standard_normal((F, C)) / np.sqrt(F)), "b2": f32(BIAS_SCALE * np.random.standard_normal((C, 1))), "offs": striped(np.random.permutation(S)[:N])}


def reference(base, x, w1, b1, w2, b2, offs):
    idx = offs[:16].T.reshape(-1)
    h = gelu_erf(f64(w1).T @ f64(x) + f64(b1))
    ff = f64(w2).T @ h + f64(b2)
    res = f64(base).copy()
    res[:, idx] = f64(x) + ff
    return res

@@ -1,0 +1,76 @@
+import concourse.mybir as mybir
+
+F32 = mybir.dt.float32
+BF16 = mybir.dt.bfloat16
+U16 = mybir.dt.uint16
+GELU = mybir.ActivationFunctionType.Gelu
+IDENTITY = mybir.ActivationFunctionType.Identity
+ADD = mybir.AluOpType.add
+
+P = 128
+C, F, S, N = 256, 1024, 4096, 512
+CB = C // P
+FB = F // P
+HALF = S // 2
+
+FLOPS = 2 * C * F * N + 2 * F * C * N
+
+
+def tile_roundencoder_kernel(tc, base, x, w1, b1, w2, b2, offs, out):
+    nc = tc.nc
+
+    x_rows = x.rearrange("(p b) n -> p b n", b=CB)
+    w1_rows = w1.rearrange("(p b) f -> p b f", b=CB)
+    w2_rows = w2.rearrange("(p t) c -> p t c", t=FB)
+    b1_rows = b1.rearrange("(p t) o -> p (t o)", t=FB)
+    b2_rows = b2.rearrange("(p b) o -> p (b o)", b=CB)
+    base_blocks = base.rearrange("(p b) s -> b p s", b=CB)
+    out_blocks = out.rearrange("(p b) s -> b p s", b=CB)
+
+    with (
+        tc.tile_pool(name="held", bufs=1) as held,
+        tc.psum_pool(name="u_banks", bufs=6) as u_banks,
+        tc.psum_pool(name="ff_banks", bufs=1) as ff_banks,
+    ):
+        x_f32 = held.tile([P, CB, N], F32, name="x_f32")
+        nc.sync.dma_start(x_f32[:], x_rows)
+        w1_sb = held.tile([P, CB, F], BF16, name="w1_sb")
+        nc.scalar.dma_start(w1_sb[:], w1_rows)
+        b1_sb = held.tile([P, FB], F32, name="b1_sb")
+        nc.scalar.dma_start(b1_sb[:], b1_rows)
+        offsets = held.tile([P, N // 16], U16, name="offsets")
+        nc.sync.dma_start(offsets[:], offs)
+        w2_sb = held.tile([P, FB, C], BF16, name="w2_sb")
+        nc.sync.dma_start(w2_sb[:], w2_rows)
+        b2_sb = held.tile([P, CB], F32, name="b2_sb")
+        nc.scalar.dma_start(b2_sb[:], b2_rows)
+        windows = [held.tile([P, S], F32, name=f"window{b}") for b in range(CB)]
+        for b in range(CB):
+            nc.sync.dma_start(windows[b][:, :HALF], base_blocks[b, :, :HALF])
+            nc.scalar.dma_start(windows[b][:, HALF:], base_blocks[b, :, HALF:])
+
+        x_bf = held.tile([P, CB, N], BF16, name="x_bf")
+        for b in range(CB):
+            nc.vector.tensor_copy(x_bf[:, b, :], x_f32[:, b, :])
+
+        w1_blocks = w1_sb[:].rearrange("k b (m t) -> k b t m", t=FB)
+        w2_blocks = w2_sb[:].rearrange("k t (m b) -> k t b m", b=CB)
+
+        h_blocks = [held.tile([P, N], BF16, name=f"h{t}") for t in range(FB)]
+        for t in range(FB):
+            u = u_banks.tile([P, N], F32, name="u")
+            for b in range(CB):
+                nc.tensor.matmul(u[:], w1_blocks[:, b, t, :], x_bf[:, b, :], start=(b == 0), stop=(b == CB - 1))
+            nc.scalar.activation(h_blocks[t][:], u[:], GELU, bias=b1_sb[:, t : t + 1])
+
+        for b in range(CB):
+            ff = ff_banks.tile([P, N], F32, name=f"ff{b}")
+            for t in range(FB):
+                nc.tensor.matmul(ff[:], w2_blocks[:, t, b, :], h_blocks[t][:], start=(t == 0), stop=(t == FB - 1))
+            ff_b2 = held.tile([P, N], F32, name=f"ff_b2_{b}")
+            nc.scalar.activation(ff_b2[:], ff[:], IDENTITY, bias=b2_sb[:, b : b + 1])
+            nc.vector.tensor_tensor(windows[b][:].indirect(offsets[:]), ff_b2[:], x_f32[:, b, :], ADD)
+
+        for b in range(CB):
+            nc.sync.dma_start(out_blocks[b, :, :HALF], windows[b][:, :HALF])
+            nc.scalar.dma_start(out_blocks[b, :, HALF:], windows[b][:, HALF:])

@@ -64,7 +64,7 @@ def tile_roundencoder_kernel(tc, base, x, w1, b1, w2, b2, offs, out):
             nc.scalar.activation(h_blocks[t][:], u[:], GELU, bias=b1_sb[:, t : t + 1])
 
         for b in range(CB):
-            ff = ff_banks.tile([P, N], F32, name=f"ff{b}")
+            ff = ff_banks.tile([P, N], F32, name="ff")
             for t in range(FB):
                 nc.tensor.matmul(ff[:], w2_blocks[:, t, b, :], h_blocks[t][:], start=(t == 0), stop=(t == FB - 1))
             ff_b2 = held.tile([P, N], F32, name=f"ff_b2_{b}")

@@ -12,6 +12,7 @@ C, F, S, N = 256, 1024, 4096, 512
 CB = C // P
 FB = F // P
 HALF = S // 2
+WARM_MATMULS = 6
 
 FLOPS = 2 * C * F * N + 2 * F * C * N
 
@@ -31,6 +32,7 @@ def tile_roundencoder_kernel(tc, base, x, w1, b1, w2, b2, offs, out):
         tc.tile_pool(name="held", bufs=1) as held,
         tc.psum_pool(name="u_banks", bufs=6) as u_banks,
         tc.psum_pool(name="ff_banks", bufs=1) as ff_banks,
+        tc.psum_pool(name="warm_banks", bufs=1) as warm_banks,
     ):
         x_f32 = held.tile([P, CB, N], F32, name="x_f32")
         nc.sync.dma_start(x_f32[:], x_rows)
@@ -44,6 +46,15 @@ def tile_roundencoder_kernel(tc, base, x, w1, b1, w2, b2, offs, out):
         nc.sync.dma_start(w2_sb[:], w2_rows)
         b2_sb = held.tile([P, CB], F32, name="b2_sb")
         nc.scalar.dma_start(b2_sb[:], b2_rows)
+
+        zeros = held.tile([P, N], BF16, name="zeros")
+        nc.vector.memset(zeros[:], 0.0)
+        gelu_of_zero = held.tile([P, 1], F32, name="gelu_of_zero")
+        nc.scalar.activation(gelu_of_zero[:], zeros[:, :1], GELU)
+        warm_bank = warm_banks.tile([P, N], F32, name="warm_bank")
+        for i in range(WARM_MATMULS):
+            nc.tensor.matmul(warm_bank[:], zeros[:, :P], zeros[:], start=True, stop=True)
+
         windows = [held.tile([P, S], F32, name=f"window{b}") for b in range(CB)]
         for b in range(CB):
             nc.sync.dma_start(windows[b][:, :HALF], base_blocks[b, :, :HALF])
@@ -73,4 +84,4 @@ def tile_roundencoder_kernel(tc, base, x, w1, b1, w2, b2, offs, out):
 
         for b in range(CB):
             nc.sync.dma_start(out_blocks[b, :, :HALF], windows[b][:, :HALF])
-            nc.scalar.dma_start(out_blocks[b, :, HALF:], windows[b][:, HALF:])
+            nc.sync.dma_start(out_blocks[b, :, HALF:], windows[b][:, HALF:])

@@ -11,8 +11,9 @@ P = 128
 C, F, S, N = 256, 1024, 4096, 512
 CB = C // P
 FB = F // P
+GROUP = FB // 2
 HALF = S // 2
-WARM_MATMULS = 6
+WARM_MATMULS = 4
 
 FLOPS = 2 * C * F * N + 2 * F * C * N
 
@@ -35,17 +36,22 @@ def tile_roundencoder_kernel(tc, base, x, w1, b1, w2, b2, offs, out):
         tc.psum_pool(name="warm_banks", bufs=1) as warm_banks,
     ):
         x_f32 = held.tile([P, CB, N], F32, name="x_f32")
-        nc.sync.dma_start(x_f32[:], x_rows)
         w1_sb = held.tile([P, CB, F], BF16, name="w1_sb")
-        nc.scalar.dma_start(w1_sb[:], w1_rows)
+        for b in range(CB):
+            nc.sync.dma_start(x_f32[:, b, :], x_rows[:, b, :])
+            nc.sync.dma_start(w1_sb[:, b, :], w1_rows[:, b, :])
         b1_sb = held.tile([P, FB], F32, name="b1_sb")
         nc.scalar.dma_start(b1_sb[:], b1_rows)
+        b2_sb = held.tile([P, CB], F32, name="b2_sb")
+        nc.scalar.dma_start(b2_sb[:], b2_rows)
         offsets = held.tile([P, N // 16], U16, name="offsets")
         nc.sync.dma_start(offsets[:], offs)
         w2_sb = held.tile([P, FB, C], BF16, name="w2_sb")
         nc.sync.dma_start(w2_sb[:], w2_rows)
-        b2_sb = held.tile([P, CB], F32, name="b2_sb")
-        nc.scalar.dma_start(b2_sb[:], b2_rows)
+        windows = [held.tile([P, S], F32, name=f"window{b}") for b in range(CB)]
+        for b in range(CB):
+            nc.sync.dma_start(windows[b][:, :HALF], base_blocks[b, :, :HALF])
+            nc.sync.dma_start(windows[b][:, HALF:], base_blocks[b, :, HALF:])
 
         zeros = held.tile([P, N], BF16, name="zeros")
         nc.vector.memset(zeros[:], 0.0)
@@ -55,11 +61,6 @@ def tile_roundencoder_kernel(tc, base, x, w1, b1, w2, b2, offs, out):
         for i in range(WARM_MATMULS):
             nc.tensor.matmul(warm_bank[:], zeros[:, :P], zeros[:], start=True, stop=True)
 
-        windows = [held.tile([P, S], F32, name=f"window{b}") for b in range(CB)]
-        for b in range(CB):
-            nc.sync.dma_start(windows[b][:, :HALF], base_blocks[b, :, :HALF])
-            nc.scalar.dma_start(windows[b][:, HALF:], base_blocks[b, :, HALF:])
-
         x_bf = held.tile([P, CB, N], BF16, name="x_bf")
         for b in range(CB):
             nc.vector.tensor_copy(x_bf[:, b, :], x_f32[:, b, :])
@@ -68,11 +69,14 @@ def tile_roundencoder_kernel(tc, base, x, w1, b1, w2, b2, offs, out):
         w2_blocks = w2_sb[:].rearrange("k t (m b) -> k t b m", b=CB)
 
         h_blocks = [held.tile([P, N], BF16, name=f"h{t}") for t in range(FB)]
-        for t in range(FB):
-            u = u_banks.tile([P, N], F32, name="u")
+        for first in range(0, FB, GROUP):
+            group = range(first, first + GROUP)
+            u = {t: u_banks.tile([P, N], F32, name="u") for t in group}
             for b in range(CB):
-                nc.tensor.matmul(u[:], w1_blocks[:, b, t, :], x_bf[:, b, :], start=(b == 0), stop=(b == CB - 1))
-            nc.scalar.activation(h_blocks[t][:], u[:], GELU, bias=b1_sb[:, t : t + 1])
+                for t in group:
+                    nc.tensor.matmul(u[t][:], w1_blocks[:, b, t, :], x_bf[:, b, :], start=(b == 0), stop=(b == CB - 1))
+            for t in group:
+                nc.scalar.activation(h_blocks[t][:], u[t][:], GELU, bias=b1_sb[:, t : t + 1])
 
         for b in range(CB):
             ff = ff_banks.tile([P, N], F32, name="ff")

@@ -13,6 +13,8 @@ CB = C // P
 FB = F // P
 GROUP = FB // 2
 HALF = S // 2
+SIDES = 2
+SIDE_N = N // SIDES
 WARM_MATMULS = 4
 
 FLOPS = 2 * C * F * N + 2 * F * C * N
@@ -33,7 +35,6 @@ def tile_roundencoder_kernel(tc, base, x, w1, b1, w2, b2, offs, out):
         tc.tile_pool(name="held", bufs=1) as held,
         tc.psum_pool(name="u_banks", bufs=6) as u_banks,
         tc.psum_pool(name="ff_banks", bufs=1) as ff_banks,
-        tc.psum_pool(name="warm_banks", bufs=1) as warm_banks,
     ):
         x_f32 = held.tile([P, CB, N], F32, name="x_f32")
         w1_sb = held.tile([P, CB, F], BF16, name="w1_sb")
@@ -57,7 +58,7 @@ def tile_roundencoder_kernel(tc, base, x, w1, b1, w2, b2, offs, out):
         nc.vector.memset(zeros[:], 0.0)
         gelu_of_zero = held.tile([P, 1], F32, name="gelu_of_zero")
         nc.scalar.activation(gelu_of_zero[:], zeros[:, :1], GELU)
-        warm_bank = warm_banks.tile([P, N], F32, name="warm_bank")
+        warm_bank = u_banks.tile([P, N], F32, name="warm_bank", tag="u")
         for i in range(WARM_MATMULS):
             nc.tensor.matmul(warm_bank[:], zeros[:, :P], zeros[:], start=True, stop=True)
 
@@ -79,11 +80,14 @@ def tile_roundencoder_kernel(tc, base, x, w1, b1, w2, b2, offs, out):
                 nc.scalar.activation(h_blocks[t][:], u[t][:], GELU, bias=b1_sb[:, t : t + 1])
 
         for b in range(CB):
-            ff = ff_banks.tile([P, N], F32, name="ff")
+            ff = [ff_banks.tile([P, SIDE_N], F32, name=f"ff_side{i}") for i in range(SIDES)]
             for t in range(FB):
-                nc.tensor.matmul(ff[:], w2_blocks[:, t, b, :], h_blocks[t][:], start=(t == 0), stop=(t == FB - 1))
+                for i in range(SIDES):
+                    side = slice(i * SIDE_N, (i + 1) * SIDE_N)
+                    nc.tensor.matmul(ff[i][:], w2_blocks[:, t, b, :], h_blocks[t][:, side], start=(t == 0), stop=(t == FB - 1))
             ff_b2 = held.tile([P, N], F32, name=f"ff_b2_{b}")
-            nc.scalar.activation(ff_b2[:], ff[:], IDENTITY, bias=b2_sb[:, b : b + 1])
+            nc.vector.tensor_scalar_add(ff_b2[:, :SIDE_N], ff[0][:], b2_sb[:, b : b + 1])
+            nc.scalar.activation(ff_b2[:, SIDE_N:], ff[1][:], IDENTITY, bias=b2_sb[:, b : b + 1])
             nc.vector.tensor_tensor(windows[b][:].indirect(offsets[:]), ff_b2[:], x_f32[:, b, :], ADD)
 
         for b in range(CB):

@@ -43,12 +43,12 @@ def tile_roundencoder_kernel(tc, base, x, w1, b1, w2, b2, offs, out):
             nc.sync.dma_start(w1_sb[:, b, :], w1_rows[:, b, :])
         b1_sb = held.tile([P, FB], F32, name="b1_sb")
         nc.scalar.dma_start(b1_sb[:], b1_rows)
-        b2_sb = held.tile([P, CB], F32, name="b2_sb")
-        nc.scalar.dma_start(b2_sb[:], b2_rows)
         offsets = held.tile([P, N // 16], U16, name="offsets")
         nc.sync.dma_start(offsets[:], offs)
         w2_sb = held.tile([P, FB, C], BF16, name="w2_sb")
         nc.sync.dma_start(w2_sb[:], w2_rows)
+        b2_sb = held.tile([P, CB], F32, name="b2_sb")
+        nc.sync.dma_start(b2_sb[:], b2_rows)
         windows = [held.tile([P, S], F32, name=f"window{b}") for b in range(CB)]
         for b in range(CB):
             nc.sync.dma_start(windows[b][:, :HALF], base_blocks[b, :, :HALF])
@@ -86,7 +86,10 @@ def tile_roundencoder_kernel(tc, base, x, w1, b1, w2, b2, offs, out):
                     side = slice(i * SIDE_N, (i + 1) * SIDE_N)
                     nc.tensor.matmul(ff[i][:], w2_blocks[:, t, b, :], h_blocks[t][:, side], start=(t == 0), stop=(t == FB - 1))
             ff_b2 = held.tile([P, N], F32, name=f"ff_b2_{b}")
-            nc.vector.tensor_scalar_add(ff_b2[:, :SIDE_N], ff[0][:], b2_sb[:, b : b + 1])
+            if b == 0:
+                nc.vector.tensor_scalar_add(ff_b2[:, :SIDE_N], ff[0][:], b2_sb[:, b : b + 1])
+            else:
+                nc.scalar.activation(ff_b2[:, :SIDE_N], ff[0][:], IDENTITY, bias=b2_sb[:, b : b + 1])
             nc.scalar.activation(ff_b2[:, SIDE_N:], ff[1][:], IDENTITY, bias=b2_sb[:, b : b + 1])
             nc.vector.tensor_tensor(windows[b][:].indirect(offsets[:]), ff_b2[:], x_f32[:, b, :], ADD)
 

@@ -11,7 +11,7 @@ P = 128
 C, F, S, N = 256, 1024, 4096, 512
 CB = C // P
 FB = F // P
-GROUP = FB // 2
+AHEAD = FB // 2
 HALF = S // 2
 SIDES = 2
 SIDE_N = N // SIDES
@@ -70,12 +70,19 @@ def tile_roundencoder_kernel(tc, base, x, w1, b1, w2, b2, offs, out):
         w2_blocks = w2_sb[:].rearrange("k t (m b) -> k t b m", b=CB)
 
         h_blocks = [held.tile([P, N], BF16, name=f"h{t}") for t in range(FB)]
-        for first in range(0, FB, GROUP):
-            group = range(first, first + GROUP)
+        groups = [range(AHEAD)] + [range(t, t + 1) for t in range(AHEAD, FB)]
+        for group in groups:
             u = {t: u_banks.tile([P, N], F32, name="u") for t in group}
-            for b in range(CB):
+            channel_blocks = list(range(CB)) if group.start == 0 else list(reversed(range(CB)))
+            for b in channel_blocks:
                 for t in group:
-                    nc.tensor.matmul(u[t][:], w1_blocks[:, b, t, :], x_bf[:, b, :], start=(b == 0), stop=(b == CB - 1))
+                    nc.tensor.matmul(
+                        u[t][:],
+                        w1_blocks[:, b, t, :],
+                        x_bf[:, b, :],
+                        start=(b == channel_blocks[0]),
+                        stop=(b == channel_blocks[-1]),
+                    )
             for t in group:
                 nc.scalar.activation(h_blocks[t][:], u[t][:], GELU, bias=b1_sb[:, t : t + 1])
 

@@ -84,7 +84,10 @@ def tile_roundencoder_kernel(tc, base, x, w1, b1, w2, b2, offs, out):
                         stop=(b == channel_blocks[-1]),
                     )
             for t in group:
-                nc.scalar.activation(h_blocks[t][:], u[t][:], GELU, bias=b1_sb[:, t : t + 1])
+                pieces = SIDES if t == FB - 1 else 1
+                for piece in range(pieces):
+                    columns = slice(piece * (N // pieces), (piece + 1) * (N // pieces))
+                    nc.scalar.activation(h_blocks[t][:, columns], u[t][:, columns], GELU, bias=b1_sb[:, t : t + 1])
 
         for b in range(CB):
             ff = [ff_banks.tile([P, SIDE_N], F32, name=f"ff_side{i}") for i in range(SIDES)]

@@ -42,7 +42,7 @@ def tile_roundencoder_kernel(tc, base, x, w1, b1, w2, b2, offs, out):
             nc.sync.dma_start(x_f32[:, b, :], x_rows[:, b, :])
             nc.sync.dma_start(w1_sb[:, b, :], w1_rows[:, b, :])
         b1_sb = held.tile([P, FB], F32, name="b1_sb")
-        nc.scalar.dma_start(b1_sb[:], b1_rows)
+        nc.sync.dma_start(b1_sb[:], b1_rows)
         offsets = held.tile([P, N // 16], U16, name="offsets")
         nc.sync.dma_start(offsets[:], offs)
         w2_sb = held.tile([P, FB, C], BF16, name="w2_sb")

@@ -104,5 +104,6 @@ def tile_roundencoder_kernel(tc, base, x, w1, b1, w2, b2, offs, out):
             nc.vector.tensor_tensor(windows[b][:].indirect(offsets[:]), ff_b2[:], x_f32[:, b, :], ADD)
 
         for b in range(CB):
+            second_queue = nc.scalar if b == CB - 1 else nc.sync
             nc.sync.dma_start(out_blocks[b, :, :HALF], windows[b][:, :HALF])
-            nc.sync.dma_start(out_blocks[b, :, HALF:], windows[b][:, HALF:])
+            second_queue.dma_start(out_blocks[b, :, HALF:], windows[b][:, HALF:])

@@ -15,7 +15,7 @@ AHEAD = FB // 2
 HALF = S // 2
 SIDES = 2
 SIDE_N = N // SIDES
-WARM_MATMULS = 4
+WARM_MATMULS = 5
 
 FLOPS = 2 * C * F * N + 2 * F * C * N
 
@@ -54,13 +54,14 @@ def tile_roundencoder_kernel(tc, base, x, w1, b1, w2, b2, offs, out):
             nc.sync.dma_start(windows[b][:, :HALF], base_blocks[b, :, :HALF])
             nc.sync.dma_start(windows[b][:, HALF:], base_blocks[b, :, HALF:])
 
-        zeros = held.tile([P, N], BF16, name="zeros")
+        zeros = held.tile([P, P], BF16, name="zeros")
         nc.vector.memset(zeros[:], 0.0)
+        repeated_zeros = zeros[:].unsqueeze(1).to_broadcast([P, N // P, P])
         gelu_of_zero = held.tile([P, 1], F32, name="gelu_of_zero")
         nc.scalar.activation(gelu_of_zero[:], zeros[:, :1], GELU)
         warm_bank = u_banks.tile([P, N], F32, name="warm_bank", tag="u")
         for i in range(WARM_MATMULS):
-            nc.tensor.matmul(warm_bank[:], zeros[:, :P], zeros[:], start=True, stop=True)
+            nc.tensor.matmul(warm_bank[:].rearrange("p (r n) -> p r n", r=N // P), zeros[:], repeated_zeros, start=True, stop=True)
 
         x_bf = held.tile([P, CB, N], BF16, name="x_bf")
         for b in range(CB):

@@ -4,7 +4,6 @@ F32 = mybir.dt.float32
 BF16 = mybir.dt.bfloat16
 U16 = mybir.dt.uint16
 GELU = mybir.ActivationFunctionType.Gelu
-IDENTITY = mybir.ActivationFunctionType.Identity
 ADD = mybir.AluOpType.add
 
 P = 128
@@ -13,8 +12,9 @@ CB = C // P
 FB = F // P
 AHEAD = FB // 2
 HALF = S // 2
-SIDES = 2
-SIDE_N = N // SIDES
+SPLIT = 256
+SIDES = [slice(0, SPLIT), slice(SPLIT, N)]
+LAG = 2
 WARM_MATMULS = 5
 
 FLOPS = 2 * C * F * N + 2 * F * C * N
@@ -54,18 +54,21 @@ def tile_roundencoder_kernel(tc, base, x, w1, b1, w2, b2, offs, out):
             nc.sync.dma_start(windows[b][:, :HALF], base_blocks[b, :, :HALF])
             nc.sync.dma_start(windows[b][:, HALF:], base_blocks[b, :, HALF:])
 
-        zeros = held.tile([P, P], BF16, name="zeros")
-        nc.vector.memset(zeros[:], 0.0)
-        repeated_zeros = zeros[:].unsqueeze(1).to_broadcast([P, N // P, P])
+        zeros = held.tile([P, 1], BF16, name="zeros")
+        nc.gpsimd.memset(zeros[:], 0.0)
         gelu_of_zero = held.tile([P, 1], F32, name="gelu_of_zero")
-        nc.scalar.activation(gelu_of_zero[:], zeros[:, :1], GELU)
+        nc.scalar.activation(gelu_of_zero[:], zeros[:], GELU)
         warm_bank = u_banks.tile([P, N], F32, name="warm_bank", tag="u")
         for i in range(WARM_MATMULS):
-            nc.tensor.matmul(warm_bank[:].rearrange("p (r n) -> p r n", r=N // P), zeros[:], repeated_zeros, start=True, stop=True)
+            nc.tensor.matmul(warm_bank[:], zeros[:].to_broadcast([P, P]), zeros[:].to_broadcast([P, N]), start=True, stop=True)
 
         x_bf = held.tile([P, CB, N], BF16, name="x_bf")
         for b in range(CB):
             nc.vector.tensor_copy(x_bf[:, b, :], x_f32[:, b, :])
+
+        x_b2 = held.tile([P, CB, N], F32, name="x_b2")
+        for b in range(CB):
+            nc.vector.tensor_scalar_add(x_b2[:, b, :], x_f32[:, b, :], b2_sb[:, b : b + 1])
 
         w1_blocks = w1_sb[:].rearrange("k b (m t) -> k b t m", t=FB)
         w2_blocks = w2_sb[:].rearrange("k t (m b) -> k t b m", b=CB)
@@ -73,36 +76,35 @@ def tile_roundencoder_kernel(tc, base, x, w1, b1, w2, b2, offs, out):
         h_blocks = [held.tile([P, N], BF16, name=f"h{t}") for t in range(FB)]
         groups = [range(AHEAD)] + [range(t, t + 1) for t in range(AHEAD, FB)]
         for group in groups:
-            u = {t: u_banks.tile([P, N], F32, name="u") for t in group}
+            parts = [(t, columns) for t in group for columns in (SIDES if t in (0, FB - 1) else [slice(0, N)])]
+            u = [u_banks.tile([P, N], F32, name="u")[:, columns] for t, columns in parts]
             channel_blocks = list(range(CB)) if group.start == 0 else list(reversed(range(CB)))
             for b in channel_blocks:
-                for t in group:
+                for u_part, (t, columns) in zip(u, parts):
                     nc.tensor.matmul(
-                        u[t][:],
+                        u_part,
                         w1_blocks[:, b, t, :],
-                        x_bf[:, b, :],
+                        x_bf[:, b, columns],
                         start=(b == channel_blocks[0]),
                         stop=(b == channel_blocks[-1]),
                     )
-            for t in group:
-                pieces = SIDES if t == FB - 1 else 1
-                for piece in range(pieces):
-                    columns = slice(piece * (N // pieces), (piece + 1) * (N // pieces))
-                    nc.scalar.activation(h_blocks[t][:, columns], u[t][:, columns], GELU, bias=b1_sb[:, t : t + 1])
+            for u_part, (t, columns) in zip(u, parts):
+                nc.scalar.activation(h_blocks[t][:, columns], u_part, GELU, bias=b1_sb[:, t : t + 1])
 
         for b in range(CB):
-            ff = [ff_banks.tile([P, SIDE_N], F32, name=f"ff_side{i}") for i in range(SIDES)]
-            for t in range(FB):
-                for i in range(SIDES):
-                    side = slice(i * SIDE_N, (i + 1) * SIDE_N)
-                    nc.tensor.matmul(ff[i][:], w2_blocks[:, t, b, :], h_blocks[t][:, side], start=(t == 0), stop=(t == FB - 1))
-            ff_b2 = held.tile([P, N], F32, name=f"ff_b2_{b}")
+            ff = [ff_banks.tile([P, side.stop - side.start], F32, name=f"ff_side{i}") for i, side in enumerate(SIDES)]
+            for step in range(FB + LAG):
+                for i, side in enumerate(SIDES):
+                    t = step - i * LAG
+                    if 0 <= t < FB:
+                        nc.tensor.matmul(ff[i][:], w2_blocks[:, t, b, :], h_blocks[t][:, side], start=(t == 0), stop=(t == FB - 1))
+            ff_sb = held.tile([P, N], F32, name=f"ff_sb{b}")
             if b == 0:
-                nc.vector.tensor_scalar_add(ff_b2[:, :SIDE_N], ff[0][:], b2_sb[:, b : b + 1])
+                nc.vector.tensor_copy(ff_sb[:, SIDES[0]], ff[0][:])
             else:
-                nc.scalar.activation(ff_b2[:, :SIDE_N], ff[0][:], IDENTITY, bias=b2_sb[:, b : b + 1])
-            nc.scalar.activation(ff_b2[:, SIDE_N:], ff[1][:], IDENTITY, bias=b2_sb[:, b : b + 1])
-            nc.vector.tensor_tensor(windows[b][:].indirect(offsets[:]), ff_b2[:], x_f32[:, b, :], ADD)
+                nc.scalar.copy(ff_sb[:, SIDES[0]], ff[0][:])
+            nc.scalar.copy(ff_sb[:, SIDES[1]], ff[1][:])
+            nc.vector.tensor_tensor(windows[b][:].indirect(offsets[:]), ff_sb[:], x_b2[:, b, :], ADD)
 
         for b in range(CB):
             second_queue = nc.scalar if b == CB - 1 else nc.sync

import concourse.mybir as mybir

F32 = mybir.dt.float32
BF16 = mybir.dt.bfloat16
U16 = mybir.dt.uint16
GELU = mybir.ActivationFunctionType.Gelu
ADD = mybir.AluOpType.add

P = 128
C, F, S, N = 256, 1024, 4096, 512
CB = C // P
FB = F // P
AHEAD = FB // 2
HALF = S // 2
SPLIT = 256
SIDES = [slice(0, SPLIT), slice(SPLIT, N)]
LAG = 2
WARM_MATMULS = 5

FLOPS = 2 * C * F * N + 2 * F * C * N


def tile_roundencoder_kernel(tc, base, x, w1, b1, w2, b2, offs, out):
    nc = tc.nc

    x_rows = x.rearrange("(p b) n -> p b n", b=CB)
    w1_rows = w1.rearrange("(p b) f -> p b f", b=CB)
    w2_rows = w2.rearrange("(p t) c -> p t c", t=FB)
    b1_rows = b1.rearrange("(p t) o -> p (t o)", t=FB)
    b2_rows = b2.rearrange("(p b) o -> p (b o)", b=CB)
    base_blocks = base.rearrange("(p b) s -> b p s", b=CB)
    out_blocks = out.rearrange("(p b) s -> b p s", b=CB)

    with (
        tc.tile_pool(name="held", bufs=1) as held,
        tc.psum_pool(name="u_banks", bufs=6) as u_banks,
        tc.psum_pool(name="ff_banks", bufs=1) as ff_banks,
    ):
        x_f32 = held.tile([P, CB, N], F32, name="x_f32")
        w1_sb = held.tile([P, CB, F], BF16, name="w1_sb")
        for b in range(CB):
            nc.sync.dma_start(x_f32[:, b, :], x_rows[:, b, :])
            nc.sync.dma_start(w1_sb[:, b, :], w1_rows[:, b, :])
        b1_sb = held.tile([P, FB], F32, name="b1_sb")
        nc.sync.dma_start(b1_sb[:], b1_rows)
        offsets = held.tile([P, N // 16], U16, name="offsets")
        nc.sync.dma_start(offsets[:], offs)
        w2_sb = held.tile([P, FB, C], BF16, name="w2_sb")
        nc.sync.dma_start(w2_sb[:], w2_rows)
        b2_sb = held.tile([P, CB], F32, name="b2_sb")
        nc.sync.dma_start(b2_sb[:], b2_rows)
        windows = [held.tile([P, S], F32, name=f"window{b}") for b in range(CB)]
        for b in range(CB):
            nc.sync.dma_start(windows[b][:, :HALF], base_blocks[b, :, :HALF])
            nc.sync.dma_start(windows[b][:, HALF:], base_blocks[b, :, HALF:])

        zeros = held.tile([P, 1], BF16, name="zeros")
        nc.gpsimd.memset(zeros[:], 0.0)
        gelu_of_zero = held.tile([P, 1], F32, name="gelu_of_zero")
        nc.scalar.activation(gelu_of_zero[:], zeros[:], GELU)
        warm_bank = u_banks.tile([P, N], F32, name="warm_bank", tag="u")
        for i in range(WARM_MATMULS):
            nc.tensor.matmul(warm_bank[:], zeros[:].to_broadcast([P, P]), zeros[:].to_broadcast([P, N]), start=True, stop=True)

        x_bf = held.tile([P, CB, N], BF16, name="x_bf")
        for b in range(CB):
            nc.vector.tensor_copy(x_bf[:, b, :], x_f32[:, b, :])

        x_b2 = held.tile([P, CB, N], F32, name="x_b2")
        for b in range(CB):
            nc.vector.tensor_scalar_add(x_b2[:, b, :], x_f32[:, b, :], b2_sb[:, b : b + 1])

        w1_blocks = w1_sb[:].rearrange("k b (m t) -> k b t m", t=FB)
        w2_blocks = w2_sb[:].rearrange("k t (m b) -> k t b m", b=CB)

        h_blocks = [held.tile([P, N], BF16, name=f"h{t}") for t in range(FB)]
        groups = [range(AHEAD)] + [range(t, t + 1) for t in range(AHEAD, FB)]
        for group in groups:
            parts = [(t, columns) for t in group for columns in (SIDES if t in (0, FB - 1) else [slice(0, N)])]
            u = [u_banks.tile([P, N], F32, name="u")[:, columns] for t, columns in parts]
            channel_blocks = list(range(CB)) if group.start == 0 else list(reversed(range(CB)))
            for b in channel_blocks:
                for u_part, (t, columns) in zip(u, parts):
                    nc.tensor.matmul(
                        u_part,
                        w1_blocks[:, b, t, :],
                        x_bf[:, b, columns],
                        start=(b == channel_blocks[0]),
                        stop=(b == channel_blocks[-1]),
                    )
            for u_part, (t, columns) in zip(u, parts):
                nc.scalar.activation(h_blocks[t][:, columns], u_part, GELU, bias=b1_sb[:, t : t + 1])

        for b in range(CB):
            ff = [ff_banks.tile([P, side.stop - side.start], F32, name=f"ff_side{i}") for i, side in enumerate(SIDES)]
            for step in range(FB + LAG):
                for i, side in enumerate(SIDES):
                    t = step - i * LAG
                    if 0 <= t < FB:
                        nc.tensor.matmul(ff[i][:], w2_blocks[:, t, b, :], h_blocks[t][:, side], start=(t == 0), stop=(t == FB - 1))
            ff_sb = held.tile([P, N], F32, name=f"ff_sb{b}")
            if b == 0:
                nc.vector.tensor_copy(ff_sb[:, SIDES[0]], ff[0][:])
            else:
                nc.scalar.copy(ff_sb[:, SIDES[0]], ff[0][:])
            nc.scalar.copy(ff_sb[:, SIDES[1]], ff[1][:])
            nc.vector.tensor_tensor(windows[b][:].indirect(offsets[:]), ff_sb[:], x_b2[:, b, :], ADD)

        for b in range(CB):
            second_queue = nc.scalar if b == CB - 1 else nc.sync
            nc.sync.dma_start(out_blocks[b, :, :HALF], windows[b][:, :HALF])
            second_queue.dma_start(out_blocks[b, :, HALF:], windows[b][:, HALF:])
